import numpy as np
import ml_dtypes


def mxq(x, axis, fmt="e4m3"):
    dtype, down = {"e4m3": (ml_dtypes.float8_e4m3fn, 7), "e5m2": (ml_dtypes.float8_e5m2, 14)}[fmt]
    v = np.moveaxis(np.asarray(x, np.float32).astype(ml_dtypes.bfloat16).astype(np.float64), axis, -1)
    blocks = v.reshape(v.shape[:-1] + (-1, 32))
    amax = np.abs(blocks).max(-1, keepdims=True)
    byte = np.maximum(np.where(amax > 0, np.frexp(amax)[1] - 1 + 127, 0) - down, 1)
    scale = np.exp2(byte - 127.0)
    codes = (blocks / scale).astype(np.float32).astype(dtype).astype(np.float64)
    return np.moveaxis((codes * scale).reshape(v.shape), -1, axis)


WIDE = False


def mx_kscale(k):
    if not WIDE:
        return np.ones(k)
    levels = np.array([30, -30])
    if k % 512:
        return np.exp2(np.random.permutation(np.resize(levels, k // 32))).repeat(32)
    a = np.empty((k // 512, 16))
    for p in range(k // 512):
        a[p, :8] = np.random.permutation(np.resize(levels, 8))
        for g in range(8):
            far = levels[np.abs(levels - a[p, g]) >= 10]
            a[p, g + 8] = far[np.random.randint(len(far))]
    return np.exp2(a.ravel()).repeat(32)


BF16 = ml_dtypes.bfloat16


def bf(x):
    return np.asarray(x, np.float32).astype(BF16)


def f64(x):
    return np.asarray(x).astype(np.float64)


B, H, W, S2, CIN, QDIM, KDIM, NH = 2, 32, 64, 256, 1024, 1024, 2048, 16
HD = QDIM // NH
D4 = HD // 4
EPS = 1e-6


def layernorm(t, g, b):
    mu = t.mean(-1, keepdims=True)
    var = ((t - mu) ** 2).mean(-1, keepdims=True)
    return (t - mu) * (1.0 / np.sqrt(var + EPS)) * g + b


def interleave(th, tw):
    return np.stack([np.broadcast_to(th[:, None, :], (H, W, D4)), np.broadcast_to(tw[None, :, :], (H, W, D4))], axis=-1).reshape(H, W, HD // 2)


def setup_inputs():
    s = mx_kscale(CIN)
    ah = np.random.uniform(-np.pi, np.pi, (H, D4))
    aw = np.random.uniform(-np.pi, np.pi, (W, D4))
    return {"x": bf(np.random.standard_normal((B, H * W, CIN)) * s),
            "wq": bf(np.random.standard_normal((QDIM, CIN)) / np.sqrt(CIN) / s[None, :]),
            "bq": bf(np.random.standard_normal(QDIM) * 0.3),
            "qn_g": bf(1.0 + 0.1 * np.random.standard_normal(HD)),
            "qn_b": bf(0.1 * np.random.standard_normal(HD)),
            "cos_h": bf(np.cos(ah)), "sin_h": bf(np.sin(ah)),
            "cos_w": bf(np.cos(aw)), "sin_w": bf(np.sin(aw))}


def reference(x, wq, bq, qn_g, qn_b, cos_h, sin_h, cos_w, sin_w):
    q = (mxq(f64(x), 2, "e5m2") @ mxq(f64(wq), 1, "e4m3").T) + f64(bq)
    q = q.reshape(B, H * W, NH, HD).transpose(0, 2, 1, 3)
    q = layernorm(q, f64(qn_g), f64(qn_b))
    cos = interleave(f64(cos_h), f64(cos_w))
    sin = interleave(f64(sin_h), f64(sin_w))
    qr = q.reshape(B, NH, H, W, HD // 2, 2)
    qe, qo = qr[..., 0], qr[..., 1]
    return np.stack([qe * cos - qo * sin, qe * sin + qo * cos], axis=-1).reshape(B, NH, H * W, HD)

@@ -1,0 +1,393 @@
+from contextlib import ExitStack
+
+import concourse.mybir as mybir
+from concourse.masks import make_identity
+
+FLOPS = 2 * 4096 * 1024 * 1024
+
+F32 = mybir.dt.float32
+BF16 = mybir.dt.bfloat16
+U32 = mybir.dt.uint32
+U8 = mybir.dt.uint8
+E5X4 = mybir.dt.float8_e5m2_x4
+E4X4 = mybir.dt.float8_e4m3fn_x4
+ALU = mybir.AluOpType
+ACT = mybir.ActivationFunctionType
+AX = mybir.AxisListType
+
+P = 128
+K = 1024
+NH = 16
+HD = 64
+NT = 32
+EPS = 1e-6
+
+
+def tile_crossattention2d_rope_pa_kernel(tc, x, wq, bq, qn_g, qn_b, cos_h, sin_h, cos_w, sin_w, out):
+    nc = tc.nc
+    with ExitStack() as ctx:
+        ctx.enter_context(tc.manual_schedule())
+        const = ctx.enter_context(tc.tile_pool(name="const", bufs=1))
+        xrp = ctx.enter_context(tc.tile_pool(name="xrp", bufs=4))
+        wrp = ctx.enter_context(tc.tile_pool(name="wrp", bufs=4))
+        wgp = ctx.enter_context(tc.tile_pool(name="wgp", bufs=2))
+        xgp = ctx.enter_context(tc.tile_pool(name="xgp", bufs=3))
+        xcp = ctx.enter_context(tc.tile_pool(name="xcp", bufs=3))
+        xsp = ctx.enter_context(tc.tile_pool(name="xsp", bufs=3))
+        tnp = ctx.enter_context(tc.tile_pool(name="tnp", bufs=2))
+        zp = ctx.enter_context(tc.tile_pool(name="zp", bufs=3))
+        m1p = ctx.enter_context(tc.tile_pool(name="m1p", bufs=3))
+        m2p = ctx.enter_context(tc.tile_pool(name="m2p", bufs=2))
+        op = ctx.enter_context(tc.tile_pool(name="op", bufs=3))
+        jap = ctx.enter_context(tc.tile_pool(name="jap", bufs=2))
+        jcp = ctx.enter_context(tc.tile_pool(name="jcp", bufs=2))
+        stp = ctx.enter_context(tc.tile_pool(name="stp", bufs=4))
+        acc0p = ctx.enter_context(tc.psum_pool(name="acc0p", bufs=2))
+        acc1p = ctx.enter_context(tc.psum_pool(name="acc1p", bufs=2))
+        xtp = ctx.enter_context(tc.psum_pool(name="xtp", bufs=2))
+        tabp = ctx.enter_context(tc.psum_pool(name="tabp", bufs=2))
+
+        ident = const.tile([P, P], F32, name="ident")
+        make_identity(nc, ident[:])
+        one = const.tile([P, 1], F32, name="one")
+        nc.vector.memset(one[:], 1.0)
+        src = const.tile([P, 1472], BF16, name="src")
+        nc.vector.memset(src[:], 0.0)
+        eps = const.tile([P, 1], F32, name="eps")
+        nc.vector.memset(eps[:], EPS)
+
+        warm = const.tile([P, 1], F32, name="warm")
+        nc.scalar.activation(out=warm[:], in_=one[:], func=ACT.Sqrt)
+        nc.gpsimd.dma_start(out=src[64:65, 448:1472], in_=bq.unsqueeze(0))
+        nc.gpsimd.dma_start(out=src[64:65, 320:384], in_=qn_g.unsqueeze(0))
+        nc.gpsimd.dma_start(out=src[64:65, 384:448], in_=qn_b.unsqueeze(0))
+        nc.scalar.dma_start(out=src[0:4, 0:128].rearrange("a (g c) -> a g c", c=16), in_=cos_h.rearrange("(g a) c -> a g c", a=4))
+        nc.scalar.dma_start(out=src[0:4, 128:256].rearrange("a (g c) -> a g c", c=16), in_=sin_h.rearrange("(g a) c -> a g c", a=4))
+        nc.scalar.dma_start(out=src[32:64, 256:288], in_=cos_w.rearrange("(q j) c -> q (j c)", j=2))
+        nc.scalar.dma_start(out=src[32:64, 288:320], in_=sin_w.rearrange("(q j) c -> q (j c)", j=2))
+
+        xr = {}
+        wr = {}
+
+        def load_w(q):
+            t = wrp.tile([P, 2, K], BF16, name="wr", tag="wr")
+            nc.sync.dma_start(out=t[:], in_=wq[256 * q : 256 * (q + 1), :].rearrange("(f p) k -> p f k", p=P))
+            wr[q] = t
+
+        def load_x(grp):
+            g8, b = grp // 2, grp % 2
+            t = xrp.tile([P, 2, K], BF16, name="xr", tag="xr")
+            nc.sync.dma_start(
+                out=t[:].rearrange("p j k -> p (j k)"),
+                in_=x[b, 256 * g8 : 256 * (g8 + 1), :].rearrange("(p j) k -> p (j k)", j=2),
+            )
+            xr[grp] = t
+
+        load_w(0)
+        load_w(1)
+        load_x(0)
+        load_w(2)
+        load_w(3)
+        load_x(1)
+        load_x(2)
+        load_x(3)
+
+        sel = const.tile([P, P], BF16, name="sel")
+        nc.vector.memset(sel[:], 0.0)
+        nc.vector.tensor_copy(
+            out=sel[32:64, :].rearrange("p (a q) -> p a q", a=4),
+            in_=ident[32:64, 32:64].unsqueeze(1).to_broadcast([32, 4, 32]),
+        )
+        nc.vector.tensor_copy(
+            out=sel[0:4, :].rearrange("p (a q) -> p a q", a=4),
+            in_=ident[0:4, 0:4].unsqueeze(2).to_broadcast([4, 4, 32]),
+        )
+        nc.vector.memset(sel[64:65, :], 1.0)
+
+        pbs = {}
+        tsb = const.tile([P, 448], F32, name="tsb")
+        ts = const.tile([P, 30, 32], F32, name="ts")
+        bc = const.tile([P, NH * HD], F32, name="bc")
+
+        def sel_block():
+            pb0 = acc0p.tile([P, 512], F32, name="pb0", tag="acc0")
+            pb1 = acc1p.tile([P, 512], F32, name="pb1", tag="acc1")
+            pt = acc0p.tile([P, 448], F32, name="pt", tag="acc0")
+            nc.tensor.matmul(out=pt[:], lhsT=sel[:], rhs=src[:, 0:448], start=True, stop=True)
+            nc.tensor.matmul(out=pb0[:], lhsT=sel[:], rhs=src[:, 448:960], start=True, stop=True)
+            nc.tensor.matmul(out=pb1[:], lhsT=sel[:], rhs=src[:, 960:1472], start=True, stop=True)
+
+            nc.scalar.copy(out=tsb[:], in_=pt[:])
+
+            pbs[0] = pb0
+            pbs[1] = pb1
+            gsw = const.tile([P, 2, 32, 2], F32, name="gsw")
+            gbv = tsb[:, 320:448].rearrange("p (w q e) -> p w q e", w=2, e=2)
+            nc.gpsimd.tensor_scalar(out=gsw[:, :, :, 0], in0=gbv[:, :, :, 1], scalar1=-1.0, scalar2=0.0, op0=ALU.mult, op1=ALU.add)
+            nc.gpsimd.tensor_scalar(out=gsw[:, :, :, 1], in0=gbv[:, :, :, 0], scalar1=1.0, scalar2=0.0, op0=ALU.mult, op1=ALU.add)
+            tmp1 = const.tile([P, 8, 32], F32, name="tmp1")
+            tmp2 = const.tile([P, 8, 32], F32, name="tmp2")
+
+            def vec(v, which, tau, n):
+                return v[:, which].rearrange("p (c t) e -> p c t e", t=2)[:, :, tau, :].unsqueeze(1).to_broadcast([P, n, 16, 2])
+
+            def ang(c0, n):
+                return tsb[:, c0 : c0 + 16 * n].rearrange("p (n c) -> p n c", c=16).unsqueeze(3).to_broadcast([P, n, 16, 2])
+
+            def pairs(ap):
+                return ap.rearrange("p n (c e) -> p n c e", e=2)
+
+            for tau, base, n, ccol, scol in ((0, 0, 8, 0, 128), (1, 24, 2, 256, 288)):
+                end = base + 3 * n
+                nc.gpsimd.tensor_tensor(out=pairs(ts[:, base + 0 : end : 3, :]), in0=ang(ccol, n), in1=vec(gbv, 0, tau, n), op=ALU.mult)
+                nc.gpsimd.tensor_tensor(out=pairs(ts[:, base + 1 : end : 3, :]), in0=ang(scol, n), in1=vec(gsw, 0, tau, n), op=ALU.mult)
+                nc.gpsimd.tensor_tensor(out=pairs(tmp1[:, 0:n, :]), in0=ang(ccol, n), in1=vec(gbv, 1, tau, n), op=ALU.mult)
+                nc.gpsimd.tensor_tensor(out=pairs(tmp2[:, 0:n, :]), in0=ang(scol, n), in1=vec(gsw, 1, tau, n), op=ALU.mult)
+                nc.gpsimd.tensor_tensor(out=ts[:, base + 2 : end : 3, :], in0=tmp1[:, 0:n, :], in1=tmp2[:, 0:n, :], op=ALU.add)
+
+
+        def bias_block():
+            sb = const.tile([P, NH], F32, name="sb")
+            nmb = const.tile([P, NH], F32, name="nmb")
+            for hf in range(2):
+                nc.vector.tensor_reduce(out=sb[:, 8 * hf : 8 * hf + 8], in_=pbs[hf][:].rearrange("p (h d) -> p h d", d=HD), axis=AX.X, op=ALU.add)
+            nc.vector.tensor_scalar_mul(out=nmb[:], in0=sb[:], scalar1=-1.0 / HD)
+            for hf in range(2):
+                nc.vector.tensor_tensor(
+                    out=bc[:, 512 * hf : 512 * (hf + 1)].rearrange("p (h d) -> p h d", d=HD),
+                    in0=pbs[hf][:].rearrange("p (h d) -> p h d", d=HD),
+                    in1=nmb[:, 8 * hf : 8 * hf + 8].unsqueeze(2).to_broadcast([P, 8, HD]),
+                    op=ALU.add,
+                )
+
+
+        wc = const.tile([P, 2, 2, 512], U32, name="wc", align_bytes=64)
+        ws = const.tile([P, 2, 2, 512], U8, name="ws", align_bytes=64)
+        wg = {}
+        xt = {}
+        xg = {}
+        xc = {}
+        xs = {}
+        acc = {}
+        sums = {}
+        nmu = {}
+        zt = {}
+        ssq = {}
+        sdv = {}
+        rst = {}
+        m1t = {}
+        m2t = {}
+        ot = {}
+        tn = {}
+        tab = {}
+
+        def transposes(key, raw):
+            t = xtp.tile([P, 4, P], F32, name="xt", tag="xt")
+            words = raw.bitcast(F32)
+            for g in range(2):
+                for u in range(2):
+                    nc.tensor.transpose(t[:, 2 * g + u, :], words[:, 256 * g + u : 256 * (g + 1) : 2], ident[:])
+            xt[key] = t
+
+        def s_wt(ft):
+            transposes(("w", ft), wr[ft // 2][:, ft % 2, :])
+
+        def s_wcopy(ft):
+            hf, fl = ft // 4, ft % 4
+            if fl == 0:
+                wg[hf] = wgp.tile([P, 2, 512, 2], F32, name="wg", tag="wg", align_bytes=64)
+            nc.scalar.copy(out=wg[hf][:, :, P * fl : P * (fl + 1), :], in_=xt[("w", ft)][:].rearrange("p (g u) f -> p g f u", u=2))
+
+        def s_wq(hf):
+            nc.vector.quantize_mx(
+                out=wc[:, hf].rearrange("p g f -> p (g f)").bitcast(E4X4),
+                scales=ws[:, hf].rearrange("p g f -> p (g f)"),
+                in_=wg[hf][:].rearrange("p g f u -> p (g f u)").bitcast(BF16),
+            )
+
+        def s_xt(t):
+            transposes(("x", t), xr[t // 2][:, t % 2, :])
+
+        def s_xcopy(t):
+            grp, j = t // 2, t % 2
+            if j == 0:
+                xg[grp] = xgp.tile([P, 2, 2, P, 2], F32, name="xg", tag="xg", align_bytes=64)
+            nc.scalar.copy(out=xg[grp][:, j], in_=xt[("x", t)][:].rearrange("p (g u) t -> p g t u", u=2))
+
+        def s_q(grp):
+            xc[grp] = xcp.tile([P, 512], U32, name="xc", tag="xc", align_bytes=64)
+            xs[grp] = xsp.tile([P, 512], U8, name="xs", tag="xs", align_bytes=64)
+            nc.vector.quantize_mx(
+                out=xc[grp][:].bitcast(E5X4),
+                scales=xs[grp][:],
+                in_=xg[grp][:].rearrange("p j g t u -> p (j g t u)").bitcast(BF16),
+            )
+
+        def s_mx(t):
+            grp, j = t // 2, t % 2
+            a0 = acc0p.tile([P, 512], F32, name="a0", tag="acc0")
+            a1 = acc1p.tile([P, 512], F32, name="a1", tag="acc1")
+            acc[t] = (a0, a1)
+            for g in range(2):
+                s = (2 * j + g) * P
+                for hf in range(2):
+                    nc.tensor.matmul_mx(
+                        out=acc[t][hf][:],
+                        lhsT=xc[grp][:, s : s + P].bitcast(E5X4),
+                        lhsT_scale=xs[grp][:, s : s + P],
+                        rhs=wc[:, hf, g, :].bitcast(E4X4),
+                        rhs_scale=ws[:, hf, g, :],
+                        start=(g == 0),
+                        stop=(g == 1),
+                    )
+
+        def hs(h):
+            return slice(HD * h, HD * (h + 1))
+
+        def s_a(t):
+            sums[t] = stp.tile([P, NH], F32, name="sums", tag="sums")
+            junk = jap.tile([P, NH * HD], BF16, name="ja", tag="ja")
+            for h in range(NH):
+                nc.scalar.activation(out=junk[:, hs(h)], in_=acc[t][h // 8][:, hs(h % 8)], func=ACT.Identity, accum_out=sums[t][:, h : h + 1])
+
+        def s_nmu(t):
+            nmu[t] = stp.tile([P, NH], F32, name="nmu", tag="nmu")
+            nc.scalar.mul(out=nmu[t][:], in_=sums[t][:], mul=-1.0 / HD)
+
+        def s_b(t):
+            zt[t] = zp.tile([P, NH * HD], F32, name="z", tag="z")
+            for h in range(NH):
+                nc.vector.scalar_tensor_tensor(
+                    out=zt[t][:, hs(h)], in0=acc[t][h // 8][:, hs(h % 8)], scalar=nmu[t][:, h : h + 1], in1=bc[:, hs(h)], op0=ALU.add, op1=ALU.add
+                )
+
+        def s_c(t):
+            ssq[t] = stp.tile([P, NH], F32, name="ssq", tag="ssq")
+            junk = jcp.tile([P, NH * HD], BF16, name="jc", tag="jc")
+            for h in range(NH):
+                nc.scalar.activation(out=junk[:, hs(h)], in_=zt[t][:, hs(h)], func=ACT.Square, accum_out=ssq[t][:, h : h + 1])
+
+        def s_sd(t):
+            sdv[t] = stp.tile([P, NH], F32, name="sdv", tag="sdv")
+            nc.scalar.activation(out=sdv[t][:], in_=ssq[t][:], func=ACT.Sqrt, bias=eps[:, 0:1], scale=1.0 / HD)
+
+        def s_recip(t):
+            rst[t] = stp.tile([P, NH], F32, name="rst", tag="rst")
+            nc.vector.reciprocal(out=rst[t][:], in_=sdv[t][:])
+
+        def s_d(t):
+            m1t[t] = m1p.tile([P, NH * HD], F32, name="m1", tag="m1")
+            nc.vector.tensor_tensor(
+                out=m1t[t][:].rearrange("p (h d) -> p h d", d=HD),
+                in0=zt[t][:].rearrange("p (h d) -> p h d", d=HD),
+                in1=tab[t // 4][:, t % 2, 0, :].unsqueeze(1).to_broadcast([P, NH, HD]),
+                op=ALU.mult,
+            )
+
+        def s_e(t):
+            m2t[t] = m2p.tile([P, NH * HD], F32, name="m2", tag="m2")
+            nc.vector.tensor_tensor(
+                out=m2t[t][:].rearrange("p (h c e) -> p h c e", h=NH, e=2),
+                in0=zt[t][:].rearrange("p (h c e) -> p h c e", h=NH, e=2)[:, :, :, ::-1],
+                in1=tab[t // 4][:, t % 2, 1, :].rearrange("p (c e) -> p c e", e=2).unsqueeze(1).to_broadcast([P, NH, 32, 2]),
+                op=ALU.mult,
+            )
+
+        def s_f(t):
+            nc.gpsimd.tensor_tensor(out=m1t[t][:], in0=m1t[t][:], in1=m2t[t][:], op=ALU.add)
+
+        def s_store(grp, half):
+            g8, b = grp // 2, grp % 2
+            nc.sync.dma_start(
+                out=out[b, 8 * half : 8 * half + 8, 256 * g8 : 256 * (g8 + 1), :].rearrange("n (p j) d -> p n (j d)", j=2),
+                in_=ot[grp][:, 8 * half : 8 * half + 8, :, :].rearrange("p n j d -> p n (j d)"),
+            )
+
+        def s_g(t):
+            grp, j = t // 2, t % 2
+            if j == 0:
+                ot[grp] = op.tile([P, NH, 2, HD], F32, name="o", tag="o")
+            for h in range(NH):
+                nc.vector.scalar_tensor_tensor(
+                    out=ot[grp][:, h, j, :], in0=m1t[t][:, hs(h)], scalar=rst[t][:, h : h + 1], in1=tab[t // 4][:, j, 2, :], op0=ALU.mult, op1=ALU.add
+                )
+                if j == 1 and h % 8 == 7:
+                    s_store(grp, h // 8)
+
+        def s_tabcopy(g8):
+            tn[g8] = tnp.tile([P, 2, 3, HD], F32, name="tn", tag="tn")
+            for j in range(2):
+                for xx in range(3):
+                    lo, hi = 3 * g8 + xx, 24 + 3 * j + xx
+                    nc.scalar.copy(
+                        out=tn[g8][:, j, xx, :].rearrange("p (c t e) -> p c t e", t=2, e=2),
+                        in_=ts[:, lo : hi + 1 : hi - lo, :].rearrange("p t (c e) -> p c t e", e=2),
+                    )
+
+        def s_tabmm(g8):
+            tab[g8] = tabp.tile([P, 2, 3, HD], F32, name="tab", tag="tab")
+            nc.tensor.matmul(
+                out=tab[g8][:].rearrange("p j x d -> p (j x d)"), lhsT=ident[:], rhs=tn[g8][:].rearrange("p j x d -> p (j x d)"), start=True, stop=True
+            )
+
+        stream = (("w", 0), ("w", 1), ("w", 2), ("w", 3), ("x", 0), ("x", 1), ("w", 4), ("w", 5), ("x", 2), ("w", 6), ("w", 7), ("x", 3))
+        prev = None
+        for k, item in enumerate(stream):
+            if item[0] == "w":
+                s_wt(item[1])
+            else:
+                s_xt(item[1])
+            if prev is not None:
+                if prev[0] == "w":
+                    s_wcopy(prev[1])
+                    if prev[1] == 3:
+                        s_wq(0)
+                        bias_block()
+                    if prev[1] == 7:
+                        s_wq(1)
+                else:
+                    s_xcopy(prev[1])
+                    if prev[1] == 1:
+                        s_q(0)
+            if k == 3:
+                sel_block()
+            prev = item
+
+        def ok(t):
+            return 0 <= t < NT
+
+        loaded = 4
+        for i in range(-3, NT + 1):
+            if ok(i + 1):
+                s_b(i + 1)
+            if ok(i + 3):
+                s_mx(i + 3)
+            if ok(i + 7):
+                s_xt(i + 7)
+            if ok(i):
+                s_c(i)
+            if ok(i + 2):
+                s_a(i + 2)
+            if ok(i):
+                s_sd(i)
+            if ok(i + 6):
+                s_xcopy(i + 6)
+            if ok(i + 2):
+                s_nmu(i + 2)
+            if (i + 2) % 4 == 0 and ok(i + 2):
+                s_tabcopy((i + 2) // 4)
+                s_tabmm((i + 2) // 4)
+            if ok(i):
+                s_d(i)
+            if i % 2 == 0 and ok(i + 4):
+                s_q((i + 4) // 2)
+            if ok(i - 1):
+                s_recip(i - 1)
+            if ok(i):
+                s_e(i)
+                s_f(i)
+            if ok(i - 1):
+                s_g(i - 1)
+            while loaded < NT // 2 and 2 * loaded - 14 <= i:
+                load_x(loaded)
+                loaded += 1

@@ -20,6 +20,7 @@ K = 1024
 NH = 16
 HD = 64
 NT = 32
+HV = 8
 EPS = 1e-6
 
 
@@ -275,12 +276,20 @@ def tile_crossattention2d_rope_pa_kernel(tc, x, wq, bq, qn_g, qn_b, cos_h, sin_h
             rst[t] = stp.tile([P, NH], F32, name="rst", tag="rst")
             nc.vector.reciprocal(out=rst[t][:], in_=sdv[t][:])
 
-        def s_d(t):
+        def s_dg(t):
             m1t[t] = m1p.tile([P, NH * HD], F32, name="m1", tag="m1")
+            nc.gpsimd.tensor_tensor(
+                out=m1t[t][:, HD * HV :].rearrange("p (h d) -> p h d", d=HD),
+                in0=zt[t][:, HD * HV :].rearrange("p (h d) -> p h d", d=HD),
+                in1=tn[t // 4][:, t % 2, 0, :].unsqueeze(1).to_broadcast([P, NH - HV, HD]),
+                op=ALU.mult,
+            )
+
+        def s_d(t):
             nc.vector.tensor_tensor(
-                out=m1t[t][:].rearrange("p (h d) -> p h d", d=HD),
-                in0=zt[t][:].rearrange("p (h d) -> p h d", d=HD),
-                in1=tab[t // 4][:, t % 2, 0, :].unsqueeze(1).to_broadcast([P, NH, HD]),
+                out=m1t[t][:, : HD * HV].rearrange("p (h d) -> p h d", d=HD),
+                in0=zt[t][:, : HD * HV].rearrange("p (h d) -> p h d", d=HD),
+                in1=tab[t // 4][:, t % 2, 0, :].unsqueeze(1).to_broadcast([P, HV, HD]),
                 op=ALU.mult,
             )
 
@@ -294,13 +303,14 @@ def tile_crossattention2d_rope_pa_kernel(tc, x, wq, bq, qn_g, qn_b, cos_h, sin_h
             )
 
         def s_f(t):
-            nc.gpsimd.tensor_tensor(out=m1t[t][:], in0=m1t[t][:], in1=m2t[t][:], op=ALU.add)
+            eng = nc.vector if t == NT - 1 else nc.gpsimd
+            eng.tensor_tensor(out=m1t[t][:], in0=m1t[t][:], in1=m2t[t][:], op=ALU.add)
 
-        def s_store(grp, half):
+        def s_store(grp, n0, n1):
             g8, b = grp // 2, grp % 2
             nc.sync.dma_start(
-                out=out[b, 8 * half : 8 * half + 8, 256 * g8 : 256 * (g8 + 1), :].rearrange("n (p j) d -> p n (j d)", j=2),
-                in_=ot[grp][:, 8 * half : 8 * half + 8, :, :].rearrange("p n j d -> p n (j d)"),
+                out=out[b, n0:n1, 256 * g8 : 256 * (g8 + 1), :].rearrange("n (p j) d -> p n (j d)", j=2),
+                in_=ot[grp][:, n0:n1, :, :].rearrange("p n j d -> p n (j d)"),
             )
 
         def s_g(t):
@@ -311,8 +321,9 @@ def tile_crossattention2d_rope_pa_kernel(tc, x, wq, bq, qn_g, qn_b, cos_h, sin_h
                 nc.vector.scalar_tensor_tensor(
                     out=ot[grp][:, h, j, :], in0=m1t[t][:, hs(h)], scalar=rst[t][:, h : h + 1], in1=tab[t // 4][:, j, 2, :], op0=ALU.mult, op1=ALU.add
                 )
-                if j == 1 and h % 8 == 7:
-                    s_store(grp, h // 8)
+                piece = 4 if t == NT - 1 else 8
+                if j == 1 and h % piece == piece - 1:
+                    s_store(grp, h + 1 - piece, h + 1)
 
         def s_tabcopy(g8):
             tn[g8] = tnp.tile([P, 2, 3, HD], F32, name="tn", tag="tn")
@@ -378,13 +389,14 @@ def tile_crossattention2d_rope_pa_kernel(tc, x, wq, bq, qn_g, qn_b, cos_h, sin_h
                 s_tabcopy((i + 2) // 4)
                 s_tabmm((i + 2) // 4)
             if ok(i):
-                s_d(i)
+                s_dg(i)
+                s_e(i)
             if i % 2 == 0 and ok(i + 4):
                 s_q((i + 4) // 2)
             if ok(i - 1):
                 s_recip(i - 1)
             if ok(i):
-                s_e(i)
+                s_d(i)
                 s_f(i)
             if ok(i - 1):
                 s_g(i - 1)

@@ -20,7 +20,8 @@ K = 1024
 NH = 16
 HD = 64
 NT = 32
-HV = 8
+HV_EVEN = 6
+HV_ODD = 4
 EPS = 1e-6
 
 
@@ -170,7 +171,6 @@ def tile_crossattention2d_rope_pa_kernel(tc, x, wq, bq, qn_g, qn_b, cos_h, sin_h
         xc = {}
         xs = {}
         acc = {}
-        sums = {}
         nmu = {}
         zt = {}
         ssq = {}
@@ -199,12 +199,14 @@ def tile_crossattention2d_rope_pa_kernel(tc, x, wq, bq, qn_g, qn_b, cos_h, sin_h
                 wg[hf] = wgp.tile([P, 2, 512, 2], F32, name="wg", tag="wg", align_bytes=64)
             nc.scalar.copy(out=wg[hf][:, :, P * fl : P * (fl + 1), :], in_=xt[("w", ft)][:].rearrange("p (g u) f -> p g f u", u=2))
 
-        def s_wq(hf):
-            nc.vector.quantize_mx(
-                out=wc[:, hf].rearrange("p g f -> p (g f)").bitcast(E4X4),
-                scales=ws[:, hf].rearrange("p g f -> p (g f)"),
-                in_=wg[hf][:].rearrange("p g f u -> p (g f u)").bitcast(BF16),
-            )
+        def s_wq(hf, fp):
+            cols = slice(256 * fp, 256 * (fp + 1))
+            for g in range(2):
+                nc.vector.quantize_mx(
+                    out=wc[:, hf, g, cols].bitcast(E4X4),
+                    scales=ws[:, hf, g, cols],
+                    in_=wg[hf][:, g, cols, :].rearrange("p f u -> p (f u)").bitcast(BF16),
+                )
 
         def s_xt(t):
             transposes(("x", t), xr[t // 2][:, t % 2, :])
@@ -229,9 +231,9 @@ def tile_crossattention2d_rope_pa_kernel(tc, x, wq, bq, qn_g, qn_b, cos_h, sin_h
             a0 = acc0p.tile([P, 512], F32, name="a0", tag="acc0")
             a1 = acc1p.tile([P, 512], F32, name="a1", tag="acc1")
             acc[t] = (a0, a1)
-            for g in range(2):
-                s = (2 * j + g) * P
-                for hf in range(2):
+            for hf in range(2):
+                for g in range(2):
+                    s = (2 * j + g) * P
                     nc.tensor.matmul_mx(
                         out=acc[t][hf][:],
                         lhsT=xc[grp][:, s : s + P].bitcast(E5X4),
@@ -246,14 +248,18 @@ def tile_crossattention2d_rope_pa_kernel(tc, x, wq, bq, qn_g, qn_b, cos_h, sin_h
             return slice(HD * h, HD * (h + 1))
 
         def s_a(t):
-            sums[t] = stp.tile([P, NH], F32, name="sums", tag="sums")
+            nmu[t] = stp.tile([P, NH], F32, name="nmu", tag="nmu")
+            if t == 0:
+                sums = stp.tile([P, NH], F32, name="sums", tag="sums")
+                for hf in range(2):
+                    nc.vector.tensor_reduce(out=sums[:, 8 * hf : 8 * hf + 8], in_=acc[t][hf][:].rearrange("p (h d) -> p h d", d=HD), axis=AX.X, op=ALU.add)
+                nc.vector.tensor_scalar_mul(out=nmu[t][:], in0=sums[:], scalar1=-1.0 / HD)
+                return
             junk = jap.tile([P, NH * HD], BF16, name="ja", tag="ja")
             for h in range(NH):
-                nc.scalar.activation(out=junk[:, hs(h)], in_=acc[t][h // 8][:, hs(h % 8)], func=ACT.Identity, accum_out=sums[t][:, h : h + 1])
-
-        def s_nmu(t):
-            nmu[t] = stp.tile([P, NH], F32, name="nmu", tag="nmu")
-            nc.scalar.mul(out=nmu[t][:], in_=sums[t][:], mul=-1.0 / HD)
+                nc.scalar.activation(
+                    out=junk[:, hs(h)], in_=acc[t][h // 8][:, hs(h % 8)], func=ACT.Copy, scale=-1.0 / HD, accum_out=nmu[t][:, h : h + 1]
+                )
 
         def s_b(t):
             zt[t] = zp.tile([P, NH * HD], F32, name="z", tag="z")
@@ -266,30 +272,32 @@ def tile_crossattention2d_rope_pa_kernel(tc, x, wq, bq, qn_g, qn_b, cos_h, sin_h
             ssq[t] = stp.tile([P, NH], F32, name="ssq", tag="ssq")
             junk = jcp.tile([P, NH * HD], BF16, name="jc", tag="jc")
             for h in range(NH):
-                nc.scalar.activation(out=junk[:, hs(h)], in_=zt[t][:, hs(h)], func=ACT.Square, accum_out=ssq[t][:, h : h + 1])
+                nc.scalar.activation(out=junk[:, hs(h)], in_=zt[t][:, hs(h)], func=ACT.Square, scale=0.125, accum_out=ssq[t][:, h : h + 1])
 
         def s_sd(t):
             sdv[t] = stp.tile([P, NH], F32, name="sdv", tag="sdv")
-            nc.scalar.activation(out=sdv[t][:], in_=ssq[t][:], func=ACT.Sqrt, bias=eps[:, 0:1], scale=1.0 / HD)
+            nc.scalar.activation(out=sdv[t][:], in_=ssq[t][:], func=ACT.Sqrt, bias=eps[:, 0:1])
 
         def s_recip(t):
             rst[t] = stp.tile([P, NH], F32, name="rst", tag="rst")
             nc.vector.reciprocal(out=rst[t][:], in_=sdv[t][:])
 
         def s_dg(t):
+            hv = HV_EVEN if t % 2 == 0 else HV_ODD
             m1t[t] = m1p.tile([P, NH * HD], F32, name="m1", tag="m1")
             nc.gpsimd.tensor_tensor(
-                out=m1t[t][:, HD * HV :].rearrange("p (h d) -> p h d", d=HD),
-                in0=zt[t][:, HD * HV :].rearrange("p (h d) -> p h d", d=HD),
-                in1=tn[t // 4][:, t % 2, 0, :].unsqueeze(1).to_broadcast([P, NH - HV, HD]),
+                out=m1t[t][:, HD * hv :].rearrange("p (h d) -> p h d", d=HD),
+                in0=zt[t][:, HD * hv :].rearrange("p (h d) -> p h d", d=HD),
+                in1=tn[t // 4][:, t % 2, 0, :].unsqueeze(1).to_broadcast([P, NH - hv, HD]),
                 op=ALU.mult,
             )
 
         def s_d(t):
+            hv = HV_EVEN if t % 2 == 0 else HV_ODD
             nc.vector.tensor_tensor(
-                out=m1t[t][:, : HD * HV].rearrange("p (h d) -> p h d", d=HD),
-                in0=zt[t][:, : HD * HV].rearrange("p (h d) -> p h d", d=HD),
-                in1=tab[t // 4][:, t % 2, 0, :].unsqueeze(1).to_broadcast([P, HV, HD]),
+                out=m1t[t][:, : HD * hv].rearrange("p (h d) -> p h d", d=HD),
+                in0=zt[t][:, : HD * hv].rearrange("p (h d) -> p h d", d=HD),
+                in1=tab[t // 4][:, t % 2, 0, :].unsqueeze(1).to_broadcast([P, hv, HD]),
                 op=ALU.mult,
             )
 
@@ -351,11 +359,10 @@ def tile_crossattention2d_rope_pa_kernel(tc, x, wq, bq, qn_g, qn_b, cos_h, sin_h
             if prev is not None:
                 if prev[0] == "w":
                     s_wcopy(prev[1])
+                    if prev[1] % 2 == 1:
+                        s_wq(prev[1] // 4, (prev[1] % 4) // 2)
                     if prev[1] == 3:
-                        s_wq(0)
                         bias_block()
-                    if prev[1] == 7:
-                        s_wq(1)
                 else:
                     s_xcopy(prev[1])
                     if prev[1] == 1:
@@ -377,14 +384,12 @@ def tile_crossattention2d_rope_pa_kernel(tc, x, wq, bq, qn_g, qn_b, cos_h, sin_h
                 s_xt(i + 7)
             if ok(i):
                 s_c(i)
-            if ok(i + 2):
+            if ok(i + 2) and i + 2 != 0:
                 s_a(i + 2)
             if ok(i):
                 s_sd(i)
             if ok(i + 6):
                 s_xcopy(i + 6)
-            if ok(i + 2):
-                s_nmu(i + 2)
             if (i + 2) % 4 == 0 and ok(i + 2):
                 s_tabcopy((i + 2) // 4)
                 s_tabmm((i + 2) // 4)
@@ -393,6 +398,8 @@ def tile_crossattention2d_rope_pa_kernel(tc, x, wq, bq, qn_g, qn_b, cos_h, sin_h
                 s_e(i)
             if i % 2 == 0 and ok(i + 4):
                 s_q((i + 4) // 2)
+            if i + 2 == 0:
+                s_a(0)
             if ok(i - 1):
                 s_recip(i - 1)
             if ok(i):

@@ -20,9 +20,10 @@ K = 1024
 NH = 16
 HD = 64
 NT = 32
-HV_EVEN = 6
-HV_ODD = 4
+HV_EVEN = 7
+HV_ODD = 5
 EPS = 1e-6
+NA_V = 2
 
 
 def tile_crossattention2d_rope_pa_kernel(tc, x, wq, bq, qn_g, qn_b, cos_h, sin_h, cos_w, sin_w, out):
@@ -59,10 +60,10 @@ def tile_crossattention2d_rope_pa_kernel(tc, x, wq, bq, qn_g, qn_b, cos_h, sin_h
         nc.vector.memset(eps[:], EPS)
 
         warm = const.tile([P, 1], F32, name="warm")
-        nc.scalar.activation(out=warm[:], in_=one[:], func=ACT.Sqrt)
-        nc.gpsimd.dma_start(out=src[64:65, 448:1472], in_=bq.unsqueeze(0))
+        nc.scalar.activation(out=warm[:], in_=one[:], func=ACT.Abs_reciprocal_sqrt)
         nc.gpsimd.dma_start(out=src[64:65, 320:384], in_=qn_g.unsqueeze(0))
         nc.gpsimd.dma_start(out=src[64:65, 384:448], in_=qn_b.unsqueeze(0))
+        nc.gpsimd.dma_start(out=src[64:65, 448:1472], in_=bq.unsqueeze(0))
         nc.scalar.dma_start(out=src[0:4, 0:128].rearrange("a (g c) -> a g c", c=16), in_=cos_h.rearrange("(g a) c -> a g c", a=4))
         nc.scalar.dma_start(out=src[0:4, 128:256].rearrange("a (g c) -> a g c", c=16), in_=sin_h.rearrange("(g a) c -> a g c", a=4))
         nc.scalar.dma_start(out=src[32:64, 256:288], in_=cos_w.rearrange("(q j) c -> q (j c)", j=2))
@@ -174,7 +175,6 @@ def tile_crossattention2d_rope_pa_kernel(tc, x, wq, bq, qn_g, qn_b, cos_h, sin_h
         nmu = {}
         zt = {}
         ssq = {}
-        sdv = {}
         rst = {}
         m1t = {}
         m2t = {}
@@ -247,13 +247,16 @@ def tile_crossattention2d_rope_pa_kernel(tc, x, wq, bq, qn_g, qn_b, cos_h, sin_h
         def hs(h):
             return slice(HD * h, HD * (h + 1))
 
+        def s_av(t, hf):
+            sums = stp.tile([P, 8], F32, name="sums", tag="sums")
+            nc.vector.tensor_reduce(out=sums[:], in_=acc[t][hf][:].rearrange("p (h d) -> p h d", d=HD), axis=AX.X, op=ALU.add)
+            nc.vector.tensor_scalar_mul(out=nmu[t][:, 8 * hf : 8 * hf + 8], in0=sums[:], scalar1=-1.0 / HD)
+
         def s_a(t):
             nmu[t] = stp.tile([P, NH], F32, name="nmu", tag="nmu")
-            if t == 0:
-                sums = stp.tile([P, NH], F32, name="sums", tag="sums")
+            if t < NA_V:
                 for hf in range(2):
-                    nc.vector.tensor_reduce(out=sums[:, 8 * hf : 8 * hf + 8], in_=acc[t][hf][:].rearrange("p (h d) -> p h d", d=HD), axis=AX.X, op=ALU.add)
-                nc.vector.tensor_scalar_mul(out=nmu[t][:], in0=sums[:], scalar1=-1.0 / HD)
+                    s_av(t, hf)
                 return
             junk = jap.tile([P, NH * HD], BF16, name="ja", tag="ja")
             for h in range(NH):
@@ -261,12 +264,19 @@ def tile_crossattention2d_rope_pa_kernel(tc, x, wq, bq, qn_g, qn_b, cos_h, sin_h
                     out=junk[:, hs(h)], in_=acc[t][h // 8][:, hs(h % 8)], func=ACT.Copy, scale=-1.0 / HD, accum_out=nmu[t][:, h : h + 1]
                 )
 
-        def s_b(t):
-            zt[t] = zp.tile([P, NH * HD], F32, name="z", tag="z")
-            for h in range(NH):
+        def s_b(t, h0=0, h1=NH):
+            if h0 == 0:
+                zt[t] = zp.tile([P, NH * HD], F32, name="z", tag="z")
+            for h in range(h0, h1):
                 nc.vector.scalar_tensor_tensor(
                     out=zt[t][:, hs(h)], in0=acc[t][h // 8][:, hs(h % 8)], scalar=nmu[t][:, h : h + 1], in1=bc[:, hs(h)], op0=ALU.add, op1=ALU.add
                 )
+
+        def s_ab0():
+            nmu[0] = stp.tile([P, NH], F32, name="nmu", tag="nmu")
+            for hf in range(2):
+                s_av(0, hf)
+                s_b(0, 8 * hf, 8 * hf + 8)
 
         def s_c(t):
             ssq[t] = stp.tile([P, NH], F32, name="ssq", tag="ssq")
@@ -275,12 +285,8 @@ def tile_crossattention2d_rope_pa_kernel(tc, x, wq, bq, qn_g, qn_b, cos_h, sin_h
                 nc.scalar.activation(out=junk[:, hs(h)], in_=zt[t][:, hs(h)], func=ACT.Square, scale=0.125, accum_out=ssq[t][:, h : h + 1])
 
         def s_sd(t):
-            sdv[t] = stp.tile([P, NH], F32, name="sdv", tag="sdv")
-            nc.scalar.activation(out=sdv[t][:], in_=ssq[t][:], func=ACT.Sqrt, bias=eps[:, 0:1])
-
-        def s_recip(t):
             rst[t] = stp.tile([P, NH], F32, name="rst", tag="rst")
-            nc.vector.reciprocal(out=rst[t][:], in_=sdv[t][:])
+            nc.scalar.activation(out=rst[t][:], in_=ssq[t][:], func=ACT.Abs_reciprocal_sqrt, bias=eps[:, 0:1])
 
         def s_dg(t):
             hv = HV_EVEN if t % 2 == 0 else HV_ODD
@@ -288,16 +294,15 @@ def tile_crossattention2d_rope_pa_kernel(tc, x, wq, bq, qn_g, qn_b, cos_h, sin_h
             nc.gpsimd.tensor_tensor(
                 out=m1t[t][:, HD * hv :].rearrange("p (h d) -> p h d", d=HD),
                 in0=zt[t][:, HD * hv :].rearrange("p (h d) -> p h d", d=HD),
-                in1=tn[t // 4][:, t % 2, 0, :].unsqueeze(1).to_broadcast([P, NH - hv, HD]),
+                in1=tn[t // 4][:, t % 2, :].unsqueeze(1).to_broadcast([P, NH - hv, HD]),
                 op=ALU.mult,
             )
 
-        def s_d(t):
-            hv = HV_EVEN if t % 2 == 0 else HV_ODD
+        def s_d(t, h0, h1):
             nc.vector.tensor_tensor(
-                out=m1t[t][:, : HD * hv].rearrange("p (h d) -> p h d", d=HD),
-                in0=zt[t][:, : HD * hv].rearrange("p (h d) -> p h d", d=HD),
-                in1=tab[t // 4][:, t % 2, 0, :].unsqueeze(1).to_broadcast([P, hv, HD]),
+                out=m1t[t][:, HD * h0 : HD * h1].rearrange("p (h d) -> p h d", d=HD),
+                in0=zt[t][:, HD * h0 : HD * h1].rearrange("p (h d) -> p h d", d=HD),
+                in1=tab[t // 4][:, t % 2, 0, :].unsqueeze(1).to_broadcast([P, h1 - h0, HD]),
                 op=ALU.mult,
             )
 
@@ -311,8 +316,7 @@ def tile_crossattention2d_rope_pa_kernel(tc, x, wq, bq, qn_g, qn_b, cos_h, sin_h
             )
 
         def s_f(t):
-            eng = nc.vector if t == NT - 1 else nc.gpsimd
-            eng.tensor_tensor(out=m1t[t][:], in0=m1t[t][:], in1=m2t[t][:], op=ALU.add)
+            nc.gpsimd.tensor_tensor(out=m1t[t][:], in0=m1t[t][:], in1=m2t[t][:], op=ALU.add)
 
         def s_store(grp, n0, n1):
             g8, b = grp // 2, grp % 2
@@ -334,22 +338,28 @@ def tile_crossattention2d_rope_pa_kernel(tc, x, wq, bq, qn_g, qn_b, cos_h, sin_h
                     s_store(grp, h + 1 - piece, h + 1)
 
         def s_tabcopy(g8):
-            tn[g8] = tnp.tile([P, 2, 3, HD], F32, name="tn", tag="tn")
+            tn[g8] = tnp.tile([P, 2, HD], F32, name="tn", tag="tn")
             for j in range(2):
-                for xx in range(3):
-                    lo, hi = 3 * g8 + xx, 24 + 3 * j + xx
-                    nc.scalar.copy(
-                        out=tn[g8][:, j, xx, :].rearrange("p (c t e) -> p c t e", t=2, e=2),
-                        in_=ts[:, lo : hi + 1 : hi - lo, :].rearrange("p t (c e) -> p c t e", e=2),
-                    )
+                lo, hi = 3 * g8, 24 + 3 * j
+                nc.scalar.copy(
+                    out=tn[g8][:, j, :].rearrange("p (c t e) -> p c t e", t=2, e=2),
+                    in_=ts[:, lo : hi + 1 : hi - lo, :].rearrange("p t (c e) -> p c t e", e=2),
+                )
 
         def s_tabmm(g8):
             tab[g8] = tabp.tile([P, 2, 3, HD], F32, name="tab", tag="tab")
-            nc.tensor.matmul(
-                out=tab[g8][:].rearrange("p j x d -> p (j x d)"), lhsT=ident[:], rhs=tn[g8][:].rearrange("p j x d -> p (j x d)"), start=True, stop=True
-            )
+            for j in range(2):
+                for xx in range(3):
+                    lo, hi = 3 * g8 + xx, 24 + 3 * j + xx
+                    nc.tensor.matmul(
+                        out=tab[g8][:, j, xx, :].rearrange("p (c t e) -> p c t e", t=2, e=2),
+                        lhsT=ident[:],
+                        rhs=ts[:, lo : hi + 1 : hi - lo, :].rearrange("p t (c e) -> p c t e", e=2),
+                        start=True,
+                        stop=True,
+                    )
 
-        stream = (("w", 0), ("w", 1), ("w", 2), ("w", 3), ("x", 0), ("x", 1), ("w", 4), ("w", 5), ("x", 2), ("w", 6), ("w", 7), ("x", 3))
+        stream = (("w", 0), ("w", 1), ("w", 2), ("w", 3), ("x", 0), ("x", 1), ("w", 4), ("w", 5), ("w", 6), ("w", 7), ("x", 2), ("x", 3))
         prev = None
         for k, item in enumerate(stream):
             if item[0] == "w":
@@ -376,7 +386,7 @@ def tile_crossattention2d_rope_pa_kernel(tc, x, wq, bq, qn_g, qn_b, cos_h, sin_h
 
         loaded = 4
         for i in range(-3, NT + 1):
-            if ok(i + 1):
+            if ok(i + 1) and i + 1 != 0:
                 s_b(i + 1)
             if ok(i + 3):
                 s_mx(i + 3)
@@ -393,18 +403,26 @@ def tile_crossattention2d_rope_pa_kernel(tc, x, wq, bq, qn_g, qn_b, cos_h, sin_h
             if (i + 2) % 4 == 0 and ok(i + 2):
                 s_tabcopy((i + 2) // 4)
                 s_tabmm((i + 2) // 4)
-            if ok(i):
+            quant = i % 2 == 0 and ok(i + 4)
+            hv = HV_EVEN if i % 2 == 0 else HV_ODD
+            if ok(i) and i != NT - 1:
                 s_dg(i)
                 s_e(i)
-            if i % 2 == 0 and ok(i + 4):
+                s_d(i, 0, hv - 1 if quant else hv)
+            if quant:
                 s_q((i + 4) // 2)
             if i + 2 == 0:
-                s_a(0)
-            if ok(i - 1):
-                s_recip(i - 1)
-            if ok(i):
-                s_d(i)
+                s_ab0()
+            if ok(i) and i != NT - 1:
+                if quant:
+                    s_d(i, hv - 1, hv)
+                if i == NT - 2:
+                    s_dg(i + 1)
                 s_f(i)
+                if i == NT - 2:
+                    s_e(i + 1)
+                    s_d(i + 1, 0, HV_ODD)
+                    s_f(i + 1)
             if ok(i - 1):
                 s_g(i - 1)
             while loaded < NT // 2 and 2 * loaded - 14 <= i:

@@ -20,8 +20,10 @@ K = 1024
 NH = 16
 HD = 64
 NT = 32
-HV_EVEN = 7
-HV_ODD = 5
+HV_EVEN = 3
+HV_ODD = 2
+KP = 5
+HG = NH - KP
 EPS = 1e-6
 NA_V = 2
 
@@ -47,7 +49,8 @@ def tile_crossattention2d_rope_pa_kernel(tc, x, wq, bq, qn_g, qn_b, cos_h, sin_h
         stp = ctx.enter_context(tc.tile_pool(name="stp", bufs=4))
         acc0p = ctx.enter_context(tc.psum_pool(name="acc0p", bufs=2))
         acc1p = ctx.enter_context(tc.psum_pool(name="acc1p", bufs=2))
-        xtp = ctx.enter_context(tc.psum_pool(name="xtp", bufs=2))
+        xtp = ctx.enter_context(tc.psum_pool(name="xtp", bufs=1))
+        msp = ctx.enter_context(tc.psum_pool(name="msp", bufs=1))
         tabp = ctx.enter_context(tc.psum_pool(name="tabp", bufs=2))
 
         ident = const.tile([P, P], F32, name="ident")
@@ -181,17 +184,21 @@ def tile_crossattention2d_rope_pa_kernel(tc, x, wq, bq, qn_g, qn_b, cos_h, sin_h
         ot = {}
         tn = {}
         tab = {}
+        ms = {}
 
-        def transposes(key, raw):
-            t = xtp.tile([P, 4, P], F32, name="xt", tag="xt")
+        def transposes(key, raw, second=False):
+            if second:
+                t = msp.tile([P, 4, P], F32, name="xtm", tag="ms")
+            else:
+                t = xtp.tile([P, 4, P], F32, name="xt", tag="xt")
             words = raw.bitcast(F32)
             for g in range(2):
                 for u in range(2):
                     nc.tensor.transpose(t[:, 2 * g + u, :], words[:, 256 * g + u : 256 * (g + 1) : 2], ident[:])
             xt[key] = t
 
-        def s_wt(ft):
-            transposes(("w", ft), wr[ft // 2][:, ft % 2, :])
+        def s_wt(ft, second=False):
+            transposes(("w", ft), wr[ft // 2][:, ft % 2, :], second)
 
         def s_wcopy(ft):
             hf, fl = ft // 4, ft % 4
@@ -208,8 +215,8 @@ def tile_crossattention2d_rope_pa_kernel(tc, x, wq, bq, qn_g, qn_b, cos_h, sin_h
                     in_=wg[hf][:, g, cols, :].rearrange("p f u -> p (f u)").bitcast(BF16),
                 )
 
-        def s_xt(t):
-            transposes(("x", t), xr[t // 2][:, t % 2, :])
+        def s_xt(t, second=False):
+            transposes(("x", t), xr[t // 2][:, t % 2, :], second)
 
         def s_xcopy(t):
             grp, j = t // 2, t % 2
@@ -316,7 +323,12 @@ def tile_crossattention2d_rope_pa_kernel(tc, x, wq, bq, qn_g, qn_b, cos_h, sin_h
             )
 
         def s_f(t):
-            nc.gpsimd.tensor_tensor(out=m1t[t][:], in0=m1t[t][:], in1=m2t[t][:], op=ALU.add)
+            nc.gpsimd.tensor_tensor(out=m1t[t][:, 0 : HD * HG], in0=m1t[t][:, 0 : HD * HG], in1=m2t[t][:, 0 : HD * HG], op=ALU.add)
+
+        def s_fp(t):
+            ms[t] = msp.tile([P, KP * HD], F32, name="ms", tag="ms")
+            nc.tensor.matmul(out=ms[t][:], lhsT=ident[:], rhs=m1t[t][:, HD * HG :], start=True, stop=False)
+            nc.tensor.matmul(out=ms[t][:], lhsT=ident[:], rhs=m2t[t][:, HD * HG :], start=False, stop=True)
 
         def s_store(grp, n0, n1):
             g8, b = grp // 2, grp % 2
@@ -329,22 +341,30 @@ def tile_crossattention2d_rope_pa_kernel(tc, x, wq, bq, qn_g, qn_b, cos_h, sin_h
             grp, j = t // 2, t % 2
             if j == 0:
                 ot[grp] = op.tile([P, NH, 2, HD], F32, name="o", tag="o")
-            for h in range(NH):
-                nc.vector.scalar_tensor_tensor(
-                    out=ot[grp][:, h, j, :], in0=m1t[t][:, hs(h)], scalar=rst[t][:, h : h + 1], in1=tab[t // 4][:, j, 2, :], op0=ALU.mult, op1=ALU.add
-                )
-                piece = 4 if t == NT - 1 else 8
-                if j == 1 and h % piece == piece - 1:
-                    s_store(grp, h + 1 - piece, h + 1)
+            piece = 4 if t == NT - 1 else 8
+            left = [piece] * (NH // piece)
+            for h in list(range(HG, NH)) + list(range(HG)):
+                if h >= HG:
+                    nc.vector.scalar_tensor_tensor(
+                        out=ot[grp][:, h, j, :], in0=ms[t][:, hs(h - HG)], scalar=rst[t][:, h : h + 1], in1=tn[t // 4][:, 2 + j, :], op0=ALU.mult, op1=ALU.add
+                    )
+                else:
+                    nc.vector.scalar_tensor_tensor(
+                        out=ot[grp][:, h, j, :], in0=m1t[t][:, hs(h)], scalar=rst[t][:, h : h + 1], in1=tab[t // 4][:, j, 2, :], op0=ALU.mult, op1=ALU.add
+                    )
+                left[h // piece] -= 1
+                if j == 1 and left[h // piece] == 0:
+                    s_store(grp, piece * (h // piece), piece * (h // piece + 1))
 
         def s_tabcopy(g8):
-            tn[g8] = tnp.tile([P, 2, HD], F32, name="tn", tag="tn")
-            for j in range(2):
-                lo, hi = 3 * g8, 24 + 3 * j
-                nc.scalar.copy(
-                    out=tn[g8][:, j, :].rearrange("p (c t e) -> p c t e", t=2, e=2),
-                    in_=ts[:, lo : hi + 1 : hi - lo, :].rearrange("p t (c e) -> p c t e", e=2),
-                )
+            tn[g8] = tnp.tile([P, 4, HD], F32, name="tn", tag="tn")
+            for xx in (0, 2):
+                for j in range(2):
+                    lo, hi = 3 * g8 + xx, 24 + 3 * j + xx
+                    nc.scalar.copy(
+                        out=tn[g8][:, xx + j, :].rearrange("p (c t e) -> p c t e", t=2, e=2),
+                        in_=ts[:, lo : hi + 1 : hi - lo, :].rearrange("p t (c e) -> p c t e", e=2),
+                    )
 
         def s_tabmm(g8):
             tab[g8] = tabp.tile([P, 2, 3, HD], F32, name="tab", tag="tab")
@@ -363,9 +383,9 @@ def tile_crossattention2d_rope_pa_kernel(tc, x, wq, bq, qn_g, qn_b, cos_h, sin_h
         prev = None
         for k, item in enumerate(stream):
             if item[0] == "w":
-                s_wt(item[1])
+                s_wt(item[1], k % 2 == 1)
             else:
-                s_xt(item[1])
+                s_xt(item[1], k % 2 == 1)
             if prev is not None:
                 if prev[0] == "w":
                     s_wcopy(prev[1])
@@ -419,12 +439,15 @@ def tile_crossattention2d_rope_pa_kernel(tc, x, wq, bq, qn_g, qn_b, cos_h, sin_h
                 if i == NT - 2:
                     s_dg(i + 1)
                 s_f(i)
+                s_fp(i)
                 if i == NT - 2:
                     s_e(i + 1)
                     s_d(i + 1, 0, HV_ODD)
                     s_f(i + 1)
             if ok(i - 1):
                 s_g(i - 1)
+            if i == NT - 1:
+                s_fp(i)
             while loaded < NT // 2 and 2 * loaded - 14 <= i:
                 load_x(loaded)
                 loaded += 1

@@ -23,7 +23,7 @@ NT = 32
 HV_EVEN = 3
 HV_ODD = 2
 KP = 5
-HG = NH - KP
+KP_END = 8
 EPS = 1e-6
 NA_V = 2
 
@@ -288,10 +288,16 @@ def tile_crossattention2d_rope_pa_kernel(tc, x, wq, bq, qn_g, qn_b, cos_h, sin_h
         def s_c(t):
             ssq[t] = stp.tile([P, NH], F32, name="ssq", tag="ssq")
             junk = jcp.tile([P, NH * HD], BF16, name="jc", tag="jc")
-            for h in range(NH):
+            if t == NT - 1:
+                rst[t] = stp.tile([P, NH], F32, name="rst", tag="rst")
+            for h in list(range(8, NH)) + list(range(8)) if t == NT - 1 else list(range(NH)):
                 nc.scalar.activation(out=junk[:, hs(h)], in_=zt[t][:, hs(h)], func=ACT.Square, scale=0.125, accum_out=ssq[t][:, h : h + 1])
+                if t == NT - 1 and h % 8 == 7:
+                    nc.scalar.activation(out=rst[t][:, h - 7 : h + 1], in_=ssq[t][:, h - 7 : h + 1], func=ACT.Abs_reciprocal_sqrt, bias=eps[:, 0:1])
 
         def s_sd(t):
+            if t == NT - 1:
+                return
             rst[t] = stp.tile([P, NH], F32, name="rst", tag="rst")
             nc.scalar.activation(out=rst[t][:], in_=ssq[t][:], func=ACT.Abs_reciprocal_sqrt, bias=eps[:, 0:1])
 
@@ -322,13 +328,24 @@ def tile_crossattention2d_rope_pa_kernel(tc, x, wq, bq, qn_g, qn_b, cos_h, sin_h
                 op=ALU.mult,
             )
 
+        def hg_of(t):
+            return NH - (KP_END if t >= NT - 2 else KP)
+
         def s_f(t):
-            nc.gpsimd.tensor_tensor(out=m1t[t][:, 0 : HD * HG], in0=m1t[t][:, 0 : HD * HG], in1=m2t[t][:, 0 : HD * HG], op=ALU.add)
+            cols = slice(0, HD * hg_of(t))
+            nc.gpsimd.tensor_tensor(out=m1t[t][:, cols], in0=m1t[t][:, cols], in1=m2t[t][:, cols], op=ALU.add)
 
         def s_fp(t):
-            ms[t] = msp.tile([P, KP * HD], F32, name="ms", tag="ms")
-            nc.tensor.matmul(out=ms[t][:], lhsT=ident[:], rhs=m1t[t][:, HD * HG :], start=True, stop=False)
-            nc.tensor.matmul(out=ms[t][:], lhsT=ident[:], rhs=m2t[t][:, HD * HG :], start=False, stop=True)
+            hg = hg_of(t)
+            kp = NH - hg
+            if t == NT - 1:
+                ms[t] = xtp.tile([P, kp * HD], F32, name="msl", tag="xt")
+            elif t == NT - 2:
+                ms[t] = acc0p.tile([P, kp * HD], F32, name="msk", tag="acc0")
+            else:
+                ms[t] = msp.tile([P, kp * HD], F32, name="ms", tag="ms")
+            nc.tensor.matmul(out=ms[t][:], lhsT=ident[:], rhs=m1t[t][:, HD * hg :], start=True, stop=False)
+            nc.tensor.matmul(out=ms[t][:], lhsT=ident[:], rhs=m2t[t][:, HD * hg :], start=False, stop=True)
 
         def s_store(grp, n0, n1):
             g8, b = grp // 2, grp % 2
@@ -343,10 +360,11 @@ def tile_crossattention2d_rope_pa_kernel(tc, x, wq, bq, qn_g, qn_b, cos_h, sin_h
                 ot[grp] = op.tile([P, NH, 2, HD], F32, name="o", tag="o")
             piece = 4 if t == NT - 1 else 8
             left = [piece] * (NH // piece)
-            for h in list(range(HG, NH)) + list(range(HG)):
-                if h >= HG:
+            hg = hg_of(t)
+            for h in list(range(hg, NH)) + list(range(hg)):
+                if h >= hg:
                     nc.vector.scalar_tensor_tensor(
-                        out=ot[grp][:, h, j, :], in0=ms[t][:, hs(h - HG)], scalar=rst[t][:, h : h + 1], in1=tn[t // 4][:, 2 + j, :], op0=ALU.mult, op1=ALU.add
+                        out=ot[grp][:, h, j, :], in0=ms[t][:, hs(h - hg)], scalar=rst[t][:, h : h + 1], in1=tn[t // 4][:, 2 + j, :], op0=ALU.mult, op1=ALU.add
                     )
                 else:
                     nc.vector.scalar_tensor_tensor(
@@ -444,10 +462,9 @@ def tile_crossattention2d_rope_pa_kernel(tc, x, wq, bq, qn_g, qn_b, cos_h, sin_h
                     s_e(i + 1)
                     s_d(i + 1, 0, HV_ODD)
                     s_f(i + 1)
+                    s_fp(i + 1)
             if ok(i - 1):
                 s_g(i - 1)
-            if i == NT - 1:
-                s_fp(i)
             while loaded < NT // 2 and 2 * loaded - 14 <= i:
                 load_x(loaded)
                 loaded += 1

@@ -430,17 +430,22 @@ def tile_crossattention2d_rope_pa_kernel(tc, x, wq, bq, qn_g, qn_b, cos_h, sin_h
                 s_mx(i + 3)
             if ok(i + 7):
                 s_xt(i + 7)
+            if i == -1:
+                s_tabmm(0)
             if ok(i):
                 s_c(i)
+            if i == 0:
+                s_xcopy(5)
             if ok(i + 2) and i + 2 != 0:
                 s_a(i + 2)
             if ok(i):
                 s_sd(i)
-            if ok(i + 6):
+            if ok(i + 6) and i != -1:
                 s_xcopy(i + 6)
             if (i + 2) % 4 == 0 and ok(i + 2):
                 s_tabcopy((i + 2) // 4)
-                s_tabmm((i + 2) // 4)
+                if i != -2:
+                    s_tabmm((i + 2) // 4)
             quant = i % 2 == 0 and ok(i + 4)
             hv = HV_EVEN if i % 2 == 0 else HV_ODD
             if ok(i) and i != NT - 1:
@@ -459,11 +464,12 @@ def tile_crossattention2d_rope_pa_kernel(tc, x, wq, bq, qn_g, qn_b, cos_h, sin_h
                 s_f(i)
                 s_fp(i)
                 if i == NT - 2:
+                    s_g(i - 1)
                     s_e(i + 1)
                     s_d(i + 1, 0, HV_ODD)
                     s_f(i + 1)
                     s_fp(i + 1)
-            if ok(i - 1):
+            if ok(i - 1) and i != NT - 2:
                 s_g(i - 1)
             while loaded < NT // 2 and 2 * loaded - 14 <= i:
                 load_x(loaded)

@@ -20,7 +20,7 @@ K = 1024
 NH = 16
 HD = 64
 NT = 32
-HV_EVEN = 3
+HV_EVEN = 4
 HV_ODD = 2
 KP = 5
 KP_END = 8

@@ -20,8 +20,8 @@ K = 1024
 NH = 16
 HD = 64
 NT = 32
-HV_EVEN = 4
-HV_ODD = 2
+HV_EVEN = 6
+HV_ODD = 0
 KP = 5
 KP_END = 8
 EPS = 1e-6
@@ -312,6 +312,8 @@ def tile_crossattention2d_rope_pa_kernel(tc, x, wq, bq, qn_g, qn_b, cos_h, sin_h
             )
 
         def s_d(t, h0, h1):
+            if h1 <= h0:
+                return
             nc.vector.tensor_tensor(
                 out=m1t[t][:, HD * h0 : HD * h1].rearrange("p (h d) -> p h d", d=HD),
                 in0=zt[t][:, HD * h0 : HD * h1].rearrange("p (h d) -> p h d", d=HD),

from contextlib import ExitStack

import concourse.mybir as mybir
from concourse.masks import make_identity

FLOPS = 2 * 4096 * 1024 * 1024

F32 = mybir.dt.float32
BF16 = mybir.dt.bfloat16
U32 = mybir.dt.uint32
U8 = mybir.dt.uint8
E5X4 = mybir.dt.float8_e5m2_x4
E4X4 = mybir.dt.float8_e4m3fn_x4
ALU = mybir.AluOpType
ACT = mybir.ActivationFunctionType
AX = mybir.AxisListType

P = 128
K = 1024
NH = 16
HD = 64
NT = 32
HV_EVEN = 6
HV_ODD = 0
KP = 5
KP_END = 8
EPS = 1e-6
NA_V = 2


def tile_crossattention2d_rope_pa_kernel(tc, x, wq, bq, qn_g, qn_b, cos_h, sin_h, cos_w, sin_w, out):
    nc = tc.nc
    with ExitStack() as ctx:
        ctx.enter_context(tc.manual_schedule())
        const = ctx.enter_context(tc.tile_pool(name="const", bufs=1))
        xrp = ctx.enter_context(tc.tile_pool(name="xrp", bufs=4))
        wrp = ctx.enter_context(tc.tile_pool(name="wrp", bufs=4))
        wgp = ctx.enter_context(tc.tile_pool(name="wgp", bufs=2))
        xgp = ctx.enter_context(tc.tile_pool(name="xgp", bufs=3))
        xcp = ctx.enter_context(tc.tile_pool(name="xcp", bufs=3))
        xsp = ctx.enter_context(tc.tile_pool(name="xsp", bufs=3))
        tnp = ctx.enter_context(tc.tile_pool(name="tnp", bufs=2))
        zp = ctx.enter_context(tc.tile_pool(name="zp", bufs=3))
        m1p = ctx.enter_context(tc.tile_pool(name="m1p", bufs=3))
        m2p = ctx.enter_context(tc.tile_pool(name="m2p", bufs=2))
        op = ctx.enter_context(tc.tile_pool(name="op", bufs=3))
        jap = ctx.enter_context(tc.tile_pool(name="jap", bufs=2))
        jcp = ctx.enter_context(tc.tile_pool(name="jcp", bufs=2))
        stp = ctx.enter_context(tc.tile_pool(name="stp", bufs=4))
        acc0p = ctx.enter_context(tc.psum_pool(name="acc0p", bufs=2))
        acc1p = ctx.enter_context(tc.psum_pool(name="acc1p", bufs=2))
        xtp = ctx.enter_context(tc.psum_pool(name="xtp", bufs=1))
        msp = ctx.enter_context(tc.psum_pool(name="msp", bufs=1))
        tabp = ctx.enter_context(tc.psum_pool(name="tabp", bufs=2))

        ident = const.tile([P, P], F32, name="ident")
        make_identity(nc, ident[:])
        one = const.tile([P, 1], F32, name="one")
        nc.vector.memset(one[:], 1.0)
        src = const.tile([P, 1472], BF16, name="src")
        nc.vector.memset(src[:], 0.0)
        eps = const.tile([P, 1], F32, name="eps")
        nc.vector.memset(eps[:], EPS)

        warm = const.tile([P, 1], F32, name="warm")
        nc.scalar.activation(out=warm[:], in_=one[:], func=ACT.Abs_reciprocal_sqrt)
        nc.gpsimd.dma_start(out=src[64:65, 320:384], in_=qn_g.unsqueeze(0))
        nc.gpsimd.dma_start(out=src[64:65, 384:448], in_=qn_b.unsqueeze(0))
        nc.gpsimd.dma_start(out=src[64:65, 448:1472], in_=bq.unsqueeze(0))
        nc.scalar.dma_start(out=src[0:4, 0:128].rearrange("a (g c) -> a g c", c=16), in_=cos_h.rearrange("(g a) c -> a g c", a=4))
        nc.scalar.dma_start(out=src[0:4, 128:256].rearrange("a (g c) -> a g c", c=16), in_=sin_h.rearrange("(g a) c -> a g c", a=4))
        nc.scalar.dma_start(out=src[32:64, 256:288], in_=cos_w.rearrange("(q j) c -> q (j c)", j=2))
        nc.scalar.dma_start(out=src[32:64, 288:320], in_=sin_w.rearrange("(q j) c -> q (j c)", j=2))

        xr = {}
        wr = {}

        def load_w(q):
            t = wrp.tile([P, 2, K], BF16, name="wr", tag="wr")
            nc.sync.dma_start(out=t[:], in_=wq[256 * q : 256 * (q + 1), :].rearrange("(f p) k -> p f k", p=P))
            wr[q] = t

        def load_x(grp):
            g8, b = grp // 2, grp % 2
            t = xrp.tile([P, 2, K], BF16, name="xr", tag="xr")
            nc.sync.dma_start(
                out=t[:].rearrange("p j k -> p (j k)"),
                in_=x[b, 256 * g8 : 256 * (g8 + 1), :].rearrange("(p j) k -> p (j k)", j=2),
            )
            xr[grp] = t

        load_w(0)
        load_w(1)
        load_x(0)
        load_w(2)
        load_w(3)
        load_x(1)
        load_x(2)
        load_x(3)

        sel = const.tile([P, P], BF16, name="sel")
        nc.vector.memset(sel[:], 0.0)
        nc.vector.tensor_copy(
            out=sel[32:64, :].rearrange("p (a q) -> p a q", a=4),
            in_=ident[32:64, 32:64].unsqueeze(1).to_broadcast([32, 4, 32]),
        )
        nc.vector.tensor_copy(
            out=sel[0:4, :].rearrange("p (a q) -> p a q", a=4),
            in_=ident[0:4, 0:4].unsqueeze(2).to_broadcast([4, 4, 32]),
        )
        nc.vector.memset(sel[64:65, :], 1.0)

        pbs = {}
        tsb = const.tile([P, 448], F32, name="tsb")
        ts = const.tile([P, 30, 32], F32, name="ts")
        bc = const.tile([P, NH * HD], F32, name="bc")

        def sel_block():
            pb0 = acc0p.tile([P, 512], F32, name="pb0", tag="acc0")
            pb1 = acc1p.tile([P, 512], F32, name="pb1", tag="acc1")
            pt = acc0p.tile([P, 448], F32, name="pt", tag="acc0")
            nc.tensor.matmul(out=pt[:], lhsT=sel[:], rhs=src[:, 0:448], start=True, stop=True)
            nc.tensor.matmul(out=pb0[:], lhsT=sel[:], rhs=src[:, 448:960], start=True, stop=True)
            nc.tensor.matmul(out=pb1[:], lhsT=sel[:], rhs=src[:, 960:1472], start=True, stop=True)

            nc.scalar.copy(out=tsb[:], in_=pt[:])

            pbs[0] = pb0
            pbs[1] = pb1
            gsw = const.tile([P, 2, 32, 2], F32, name="gsw")
            gbv = tsb[:, 320:448].rearrange("p (w q e) -> p w q e", w=2, e=2)
            nc.gpsimd.tensor_scalar(out=gsw[:, :, :, 0], in0=gbv[:, :, :, 1], scalar1=-1.0, scalar2=0.0, op0=ALU.mult, op1=ALU.add)
            nc.gpsimd.tensor_scalar(out=gsw[:, :, :, 1], in0=gbv[:, :, :, 0], scalar1=1.0, scalar2=0.0, op0=ALU.mult, op1=ALU.add)
            tmp1 = const.tile([P, 8, 32], F32, name="tmp1")
            tmp2 = const.tile([P, 8, 32], F32, name="tmp2")

            def vec(v, which, tau, n):
                return v[:, which].rearrange("p (c t) e -> p c t e", t=2)[:, :, tau, :].unsqueeze(1).to_broadcast([P, n, 16, 2])

            def ang(c0, n):
                return tsb[:, c0 : c0 + 16 * n].rearrange("p (n c) -> p n c", c=16).unsqueeze(3).to_broadcast([P, n, 16, 2])

            def pairs(ap):
                return ap.rearrange("p n (c e) -> p n c e", e=2)

            for tau, base, n, ccol, scol in ((0, 0, 8, 0, 128), (1, 24, 2, 256, 288)):
                end = base + 3 * n
                nc.gpsimd.tensor_tensor(out=pairs(ts[:, base + 0 : end : 3, :]), in0=ang(ccol, n), in1=vec(gbv, 0, tau, n), op=ALU.mult)
                nc.gpsimd.tensor_tensor(out=pairs(ts[:, base + 1 : end : 3, :]), in0=ang(scol, n), in1=vec(gsw, 0, tau, n), op=ALU.mult)
                nc.gpsimd.tensor_tensor(out=pairs(tmp1[:, 0:n, :]), in0=ang(ccol, n), in1=vec(gbv, 1, tau, n), op=ALU.mult)
                nc.gpsimd.tensor_tensor(out=pairs(tmp2[:, 0:n, :]), in0=ang(scol, n), in1=vec(gsw, 1, tau, n), op=ALU.mult)
                nc.gpsimd.tensor_tensor(out=ts[:, base + 2 : end : 3, :], in0=tmp1[:, 0:n, :], in1=tmp2[:, 0:n, :], op=ALU.add)


        def bias_block():
            sb = const.tile([P, NH], F32, name="sb")
            nmb = const.tile([P, NH], F32, name="nmb")
            for hf in range(2):
                nc.vector.tensor_reduce(out=sb[:, 8 * hf : 8 * hf + 8], in_=pbs[hf][:].rearrange("p (h d) -> p h d", d=HD), axis=AX.X, op=ALU.add)
            nc.vector.tensor_scalar_mul(out=nmb[:], in0=sb[:], scalar1=-1.0 / HD)
            for hf in range(2):
                nc.vector.tensor_tensor(
                    out=bc[:, 512 * hf : 512 * (hf + 1)].rearrange("p (h d) -> p h d", d=HD),
                    in0=pbs[hf][:].rearrange("p (h d) -> p h d", d=HD),
                    in1=nmb[:, 8 * hf : 8 * hf + 8].unsqueeze(2).to_broadcast([P, 8, HD]),
                    op=ALU.add,
                )


        wc = const.tile([P, 2, 2, 512], U32, name="wc", align_bytes=64)
        ws = const.tile([P, 2, 2, 512], U8, name="ws", align_bytes=64)
        wg = {}
        xt = {}
        xg = {}
        xc = {}
        xs = {}
        acc = {}
        nmu = {}
        zt = {}
        ssq = {}
        rst = {}
        m1t = {}
        m2t = {}
        ot = {}
        tn = {}
        tab = {}
        ms = {}

        def transposes(key, raw, second=False):
            if second:
                t = msp.tile([P, 4, P], F32, name="xtm", tag="ms")
            else:
                t = xtp.tile([P, 4, P], F32, name="xt", tag="xt")
            words = raw.bitcast(F32)
            for g in range(2):
                for u in range(2):
                    nc.tensor.transpose(t[:, 2 * g + u, :], words[:, 256 * g + u : 256 * (g + 1) : 2], ident[:])
            xt[key] = t

        def s_wt(ft, second=False):
            transposes(("w", ft), wr[ft // 2][:, ft % 2, :], second)

        def s_wcopy(ft):
            hf, fl = ft // 4, ft % 4
            if fl == 0:
                wg[hf] = wgp.tile([P, 2, 512, 2], F32, name="wg", tag="wg", align_bytes=64)
            nc.scalar.copy(out=wg[hf][:, :, P * fl : P * (fl + 1), :], in_=xt[("w", ft)][:].rearrange("p (g u) f -> p g f u", u=2))

        def s_wq(hf, fp):
            cols = slice(256 * fp, 256 * (fp + 1))
            for g in range(2):
                nc.vector.quantize_mx(
                    out=wc[:, hf, g, cols].bitcast(E4X4),
                    scales=ws[:, hf, g, cols],
                    in_=wg[hf][:, g, cols, :].rearrange("p f u -> p (f u)").bitcast(BF16),
                )

        def s_xt(t, second=False):
            transposes(("x", t), xr[t // 2][:, t % 2, :], second)

        def s_xcopy(t):
            grp, j = t // 2, t % 2
            if j == 0:
                xg[grp] = xgp.tile([P, 2, 2, P, 2], F32, name="xg", tag="xg", align_bytes=64)
            nc.scalar.copy(out=xg[grp][:, j], in_=xt[("x", t)][:].rearrange("p (g u) t -> p g t u", u=2))

        def s_q(grp):
            xc[grp] = xcp.tile([P, 512], U32, name="xc", tag="xc", align_bytes=64)
            xs[grp] = xsp.tile([P, 512], U8, name="xs", tag="xs", align_bytes=64)
            nc.vector.quantize_mx(
                out=xc[grp][:].bitcast(E5X4),
                scales=xs[grp][:],
                in_=xg[grp][:].rearrange("p j g t u -> p (j g t u)").bitcast(BF16),
            )

        def s_mx(t):
            grp, j = t // 2, t % 2
            a0 = acc0p.tile([P, 512], F32, name="a0", tag="acc0")
            a1 = acc1p.tile([P, 512], F32, name="a1", tag="acc1")
            acc[t] = (a0, a1)
            for hf in range(2):
                for g in range(2):
                    s = (2 * j + g) * P
                    nc.tensor.matmul_mx(
                        out=acc[t][hf][:],
                        lhsT=xc[grp][:, s : s + P].bitcast(E5X4),
                        lhsT_scale=xs[grp][:, s : s + P],
                        rhs=wc[:, hf, g, :].bitcast(E4X4),
                        rhs_scale=ws[:, hf, g, :],
                        start=(g == 0),
                        stop=(g == 1),
                    )

        def hs(h):
            return slice(HD * h, HD * (h + 1))

        def s_av(t, hf):
            sums = stp.tile([P, 8], F32, name="sums", tag="sums")
            nc.vector.tensor_reduce(out=sums[:], in_=acc[t][hf][:].rearrange("p (h d) -> p h d", d=HD), axis=AX.X, op=ALU.add)
            nc.vector.tensor_scalar_mul(out=nmu[t][:, 8 * hf : 8 * hf + 8], in0=sums[:], scalar1=-1.0 / HD)

        def s_a(t):
            nmu[t] = stp.tile([P, NH], F32, name="nmu", tag="nmu")
            if t < NA_V:
                for hf in range(2):
                    s_av(t, hf)
                return
            junk = jap.tile([P, NH * HD], BF16, name="ja", tag="ja")
            for h in range(NH):
                nc.scalar.activation(
                    out=junk[:, hs(h)], in_=acc[t][h // 8][:, hs(h % 8)], func=ACT.Copy, scale=-1.0 / HD, accum_out=nmu[t][:, h : h + 1]
                )

        def s_b(t, h0=0, h1=NH):
            if h0 == 0:
                zt[t] = zp.tile([P, NH * HD], F32, name="z", tag="z")
            for h in range(h0, h1):
                nc.vector.scalar_tensor_tensor(
                    out=zt[t][:, hs(h)], in0=acc[t][h // 8][:, hs(h % 8)], scalar=nmu[t][:, h : h + 1], in1=bc[:, hs(h)], op0=ALU.add, op1=ALU.add
                )

        def s_ab0():
            nmu[0] = stp.tile([P, NH], F32, name="nmu", tag="nmu")
            for hf in range(2):
                s_av(0, hf)
                s_b(0, 8 * hf, 8 * hf + 8)

        def s_c(t):
            ssq[t] = stp.tile([P, NH], F32, name="ssq", tag="ssq")
            junk = jcp.tile([P, NH * HD], BF16, name="jc", tag="jc")
            if t == NT - 1:
                rst[t] = stp.tile([P, NH], F32, name="rst", tag="rst")
            for h in list(range(8, NH)) + list(range(8)) if t == NT - 1 else list(range(NH)):
                nc.scalar.activation(out=junk[:, hs(h)], in_=zt[t][:, hs(h)], func=ACT.Square, scale=0.125, accum_out=ssq[t][:, h : h + 1])
                if t == NT - 1 and h % 8 == 7:
                    nc.scalar.activation(out=rst[t][:, h - 7 : h + 1], in_=ssq[t][:, h - 7 : h + 1], func=ACT.Abs_reciprocal_sqrt, bias=eps[:, 0:1])

        def s_sd(t):
            if t == NT - 1:
                return
            rst[t] = stp.tile([P, NH], F32, name="rst", tag="rst")
            nc.scalar.activation(out=rst[t][:], in_=ssq[t][:], func=ACT.Abs_reciprocal_sqrt, bias=eps[:, 0:1])

        def s_dg(t):
            hv = HV_EVEN if t % 2 == 0 else HV_ODD
            m1t[t] = m1p.tile([P, NH * HD], F32, name="m1", tag="m1")
            nc.gpsimd.tensor_tensor(
                out=m1t[t][:, HD * hv :].rearrange("p (h d) -> p h d", d=HD),
                in0=zt[t][:, HD * hv :].rearrange("p (h d) -> p h d", d=HD),
                in1=tn[t // 4][:, t % 2, :].unsqueeze(1).to_broadcast([P, NH - hv, HD]),
                op=ALU.mult,
            )

        def s_d(t, h0, h1):
            if h1 <= h0:
                return
            nc.vector.tensor_tensor(
                out=m1t[t][:, HD * h0 : HD * h1].rearrange("p (h d) -> p h d", d=HD),
                in0=zt[t][:, HD * h0 : HD * h1].rearrange("p (h d) -> p h d", d=HD),
                in1=tab[t // 4][:, t % 2, 0, :].unsqueeze(1).to_broadcast([P, h1 - h0, HD]),
                op=ALU.mult,
            )

        def s_e(t):
            m2t[t] = m2p.tile([P, NH * HD], F32, name="m2", tag="m2")
            nc.vector.tensor_tensor(
                out=m2t[t][:].rearrange("p (h c e) -> p h c e", h=NH, e=2),
                in0=zt[t][:].rearrange("p (h c e) -> p h c e", h=NH, e=2)[:, :, :, ::-1],
                in1=tab[t // 4][:, t % 2, 1, :].rearrange("p (c e) -> p c e", e=2).unsqueeze(1).to_broadcast([P, NH, 32, 2]),
                op=ALU.mult,
            )

        def hg_of(t):
            return NH - (KP_END if t >= NT - 2 else KP)

        def s_f(t):
            cols = slice(0, HD * hg_of(t))
            nc.gpsimd.tensor_tensor(out=m1t[t][:, cols], in0=m1t[t][:, cols], in1=m2t[t][:, cols], op=ALU.add)

        def s_fp(t):
            hg = hg_of(t)
            kp = NH - hg
            if t == NT - 1:
                ms[t] = xtp.tile([P, kp * HD], F32, name="msl", tag="xt")
            elif t == NT - 2:
                ms[t] = acc0p.tile([P, kp * HD], F32, name="msk", tag="acc0")
            else:
                ms[t] = msp.tile([P, kp * HD], F32, name="ms", tag="ms")
            nc.tensor.matmul(out=ms[t][:], lhsT=ident[:], rhs=m1t[t][:, HD * hg :], start=True, stop=False)
            nc.tensor.matmul(out=ms[t][:], lhsT=ident[:], rhs=m2t[t][:, HD * hg :], start=False, stop=True)

        def s_store(grp, n0, n1):
            g8, b = grp // 2, grp % 2
            nc.sync.dma_start(
                out=out[b, n0:n1, 256 * g8 : 256 * (g8 + 1), :].rearrange("n (p j) d -> p n (j d)", j=2),
                in_=ot[grp][:, n0:n1, :, :].rearrange("p n j d -> p n (j d)"),
            )

        def s_g(t):
            grp, j = t // 2, t % 2
            if j == 0:
                ot[grp] = op.tile([P, NH, 2, HD], F32, name="o", tag="o")
            piece = 4 if t == NT - 1 else 8
            left = [piece] * (NH // piece)
            hg = hg_of(t)
            for h in list(range(hg, NH)) + list(range(hg)):
                if h >= hg:
                    nc.vector.scalar_tensor_tensor(
                        out=ot[grp][:, h, j, :], in0=ms[t][:, hs(h - hg)], scalar=rst[t][:, h : h + 1], in1=tn[t // 4][:, 2 + j, :], op0=ALU.mult, op1=ALU.add
                    )
                else:
                    nc.vector.scalar_tensor_tensor(
                        out=ot[grp][:, h, j, :], in0=m1t[t][:, hs(h)], scalar=rst[t][:, h : h + 1], in1=tab[t // 4][:, j, 2, :], op0=ALU.mult, op1=ALU.add
                    )
                left[h // piece] -= 1
                if j == 1 and left[h // piece] == 0:
                    s_store(grp, piece * (h // piece), piece * (h // piece + 1))

        def s_tabcopy(g8):
            tn[g8] = tnp.tile([P, 4, HD], F32, name="tn", tag="tn")
            for xx in (0, 2):
                for j in range(2):
                    lo, hi = 3 * g8 + xx, 24 + 3 * j + xx
                    nc.scalar.copy(
                        out=tn[g8][:, xx + j, :].rearrange("p (c t e) -> p c t e", t=2, e=2),
                        in_=ts[:, lo : hi + 1 : hi - lo, :].rearrange("p t (c e) -> p c t e", e=2),
                    )

        def s_tabmm(g8):
            tab[g8] = tabp.tile([P, 2, 3, HD], F32, name="tab", tag="tab")
            for j in range(2):
                for xx in range(3):
                    lo, hi = 3 * g8 + xx, 24 + 3 * j + xx
                    nc.tensor.matmul(
                        out=tab[g8][:, j, xx, :].rearrange("p (c t e) -> p c t e", t=2, e=2),
                        lhsT=ident[:],
                        rhs=ts[:, lo : hi + 1 : hi - lo, :].rearrange("p t (c e) -> p c t e", e=2),
                        start=True,
                        stop=True,
                    )

        stream = (("w", 0), ("w", 1), ("w", 2), ("w", 3), ("x", 0), ("x", 1), ("w", 4), ("w", 5), ("w", 6), ("w", 7), ("x", 2), ("x", 3))
        prev = None
        for k, item in enumerate(stream):
            if item[0] == "w":
                s_wt(item[1], k % 2 == 1)
            else:
                s_xt(item[1], k % 2 == 1)
            if prev is not None:
                if prev[0] == "w":
                    s_wcopy(prev[1])
                    if prev[1] % 2 == 1:
                        s_wq(prev[1] // 4, (prev[1] % 4) // 2)
                    if prev[1] == 3:
                        bias_block()
                else:
                    s_xcopy(prev[1])
                    if prev[1] == 1:
                        s_q(0)
            if k == 3:
                sel_block()
            prev = item

        def ok(t):
            return 0 <= t < NT

        loaded = 4
        for i in range(-3, NT + 1):
            if ok(i + 1) and i + 1 != 0:
                s_b(i + 1)
            if ok(i + 3):
                s_mx(i + 3)
            if ok(i + 7):
                s_xt(i + 7)
            if i == -1:
                s_tabmm(0)
            if ok(i):
                s_c(i)
            if i == 0:
                s_xcopy(5)
            if ok(i + 2) and i + 2 != 0:
                s_a(i + 2)
            if ok(i):
                s_sd(i)
            if ok(i + 6) and i != -1:
                s_xcopy(i + 6)
            if (i + 2) % 4 == 0 and ok(i + 2):
                s_tabcopy((i + 2) // 4)
                if i != -2:
                    s_tabmm((i + 2) // 4)
            quant = i % 2 == 0 and ok(i + 4)
            hv = HV_EVEN if i % 2 == 0 else HV_ODD
            if ok(i) and i != NT - 1:
                s_dg(i)
                s_e(i)
                s_d(i, 0, hv - 1 if quant else hv)
            if quant:
                s_q((i + 4) // 2)
            if i + 2 == 0:
                s_ab0()
            if ok(i) and i != NT - 1:
                if quant:
                    s_d(i, hv - 1, hv)
                if i == NT - 2:
                    s_dg(i + 1)
                s_f(i)
                s_fp(i)
                if i == NT - 2:
                    s_g(i - 1)
                    s_e(i + 1)
                    s_d(i + 1, 0, HV_ODD)
                    s_f(i + 1)
                    s_fp(i + 1)
            if ok(i - 1) and i != NT - 2:
                s_g(i - 1)
            while loaded < NT // 2 and 2 * loaded - 14 <= i:
                load_x(loaded)
                loaded += 1
